import numpy as np
import ml_dtypes


def mxq(x, axis, fmt="e4m3"):
    dtype, down = {"e4m3": (ml_dtypes.float8_e4m3fn, 7), "e5m2": (ml_dtypes.float8_e5m2, 14)}[fmt]
    v = np.moveaxis(np.asarray(x, np.float32).astype(ml_dtypes.bfloat16).astype(np.float64), axis, -1)
    blocks = v.reshape(v.shape[:-1] + (-1, 32))
    amax = np.abs(blocks).max(-1, keepdims=True)
    byte = np.maximum(np.where(amax > 0, np.frexp(amax)[1] - 1 + 127, 0) - down, 1)
    scale = np.exp2(byte - 127.0)
    codes = (blocks / scale).astype(np.float32).astype(dtype).astype(np.float64)
    return np.moveaxis((codes * scale).reshape(v.shape), -1, axis)


WIDE = False


def mx_kscale(k):
    if not WIDE:
        return np.ones(k)
    levels = np.array([10, -10, 5, -5, 0])
    a = np.random.permutation(np.resize(levels, k // 512 * 4)).reshape(k // 512, 4)
    idx = np.arange(k)
    return np.exp2(a[idx // 512, idx % 128 // 32])


BF16 = ml_dtypes.bfloat16


def bf(x):
    return np.asarray(x, np.float32).astype(BF16)


def f64(x):
    return np.asarray(x).astype(np.float64)


N_FFT, B, T = 512, 16, 256
STRIDE = N_FFT + 1
L = T * STRIDE


def _fourier_kernels(n_fft):
    s = np.arange(n_fft, dtype=np.float64)
    k = np.arange(n_fft, dtype=np.float64)[:, None]
    ang = 2.0 * np.pi * k * s / n_fft
    return np.sin(ang), np.cos(ang)


def setup_inputs():
    s = mx_kscale(N_FFT)
    sx = np.concatenate([s, np.ones(1)])
    x = (np.random.standard_normal((1, B, T, STRIDE)) * sx).reshape(1, B, L)
    ws, wc = _fourier_kernels(N_FFT)
    wsin = (ws + 0.5 * np.random.standard_normal((N_FFT, N_FFT))) / np.sqrt(N_FFT) / s[None, :]
    wcos = (wc + 0.5 * np.random.standard_normal((N_FFT, N_FFT))) / np.sqrt(N_FFT) / s[None, :]
    return {"x": bf(x), "wsin": bf(wsin), "wcos": bf(wcos)}


def reference(x, wsin, wcos):
    sig = f64(x)[0]
    frames = sig.reshape(B, T, STRIDE)[..., :N_FFT]
    fq = mxq(frames, 2, "e4m3")
    real = np.einsum('btn,kn->tbk', fq, mxq(f64(wcos), 1, "e4m3"))
    imag = np.einsum('btn,kn->tbk', fq, mxq(f64(wsin), 1, "e4m3"))
    return real, -imag

@@ -1,0 +1,118 @@
+from contextlib import ExitStack
+
+import concourse.mybir as mybir
+from concourse.masks import make_identity
+
+F32 = mybir.dt.float32
+BF16 = mybir.dt.bfloat16
+U32 = mybir.dt.uint32
+U8 = mybir.dt.uint8
+FP8X4 = mybir.dt.float8_e4m3fn_x4
+
+P = 128
+N_FFT = 512
+SIGNALS = 16
+FRAMES = 256
+STRIDE = N_FFT + 1
+PACK = 4
+WORDS = N_FFT // 2
+HALVES = WORDS // P
+GROUP = 4
+HALF_FRAMES = FRAMES // P
+CHUNKS = HALF_FRAMES * SIGNALS // GROUP
+
+FLOPS = 2 * SIGNALS * FRAMES * N_FFT * (2 * N_FFT)
+
+
+def quantise_group(nc, pools, rows, ident):
+    grouped = pools["grouped"].tile([P, GROUP * P * PACK], BF16, align_bytes=64)
+    grouped_words = grouped[:].bitcast(F32).rearrange("p (a r u) -> p a r u", a=GROUP, u=HALVES)
+    for pair in range(GROUP // 2):
+        flipped = pools["flipped"].tile([P, 2, HALVES, P], F32)
+        for a in range(2):
+            row_words = rows[:, 2 * pair + a, :].bitcast(F32)
+            for u in range(HALVES):
+                nc.tensor.transpose(flipped[:, a, u, :], row_words[:, u * P : (u + 1) * P], ident[:])
+        source = flipped[:].rearrange("p a u r -> p a r u")
+        target = grouped_words[:, 2 * pair : 2 * pair + 2, :, :]
+        if pair % 2 == 0:
+            nc.scalar.copy(out=target, in_=source)
+        else:
+            nc.vector.tensor_copy(out=target, in_=source)
+    codes = pools["codes"].tile([P, GROUP * P], U32, align_bytes=64)
+    scales = pools["scales"].tile([P, GROUP * P], U8, align_bytes=64)
+    nc.vector.quantize_mx(out=codes[:].bitcast(FP8X4), scales=scales[:], in_=grouped[:])
+    return codes, scales
+
+
+def tile_dftlayer_t_kernel(tc, x, wsin, wcos, out_0, out_1):
+    nc = tc.nc
+    with ExitStack() as ctx:
+        pools = {
+            "rows": ctx.enter_context(tc.tile_pool(name="rows", bufs=2 + CHUNKS)),
+            "const": ctx.enter_context(tc.tile_pool(name="const", bufs=1)),
+            "grouped": ctx.enter_context(tc.tile_pool(name="grouped", bufs=3)),
+            "codes": ctx.enter_context(tc.tile_pool(name="codes", bufs=2 + 3)),
+            "scales": ctx.enter_context(tc.tile_pool(name="scales", bufs=2 + 3)),
+            "results": ctx.enter_context(tc.tile_pool(name="results", bufs=CHUNKS)),
+            "flipped": ctx.enter_context(tc.psum_pool(name="flipped", bufs=2)),
+            "product": ctx.enter_context(tc.psum_pool(name="product", bufs=6)),
+        }
+
+        weight_rows = []
+        for w in (wcos, wsin):
+            rows = pools["rows"].tile([P, GROUP, N_FFT], BF16, tag="rows", name="w_rows")
+            nc.sync.dma_start(out=rows[:], in_=w.rearrange("(a p) n -> p a n", p=P))
+            weight_rows.append(rows)
+        pieces = x[0].rearrange("b (t s) -> t b s", s=STRIDE)
+        frame_rows = []
+        for c in range(CHUNKS):
+            half, b0 = c // (SIGNALS // GROUP), GROUP * (c % (SIGNALS // GROUP))
+            rows = pools["rows"].tile([P, GROUP, N_FFT], BF16, tag="rows", name="x_rows")
+            nc.sync.dma_start(
+                out=rows[:], in_=pieces[half * P : (half + 1) * P, b0 : b0 + GROUP, 0:N_FFT]
+            )
+            frame_rows.append(rows)
+
+        ident = pools["const"].tile([P, P], F32)
+        make_identity(nc, ident[:])
+
+        cos_codes, cos_scales = quantise_group(nc, pools, weight_rows[0], ident)
+        sin_codes, sin_scales = quantise_group(nc, pools, weight_rows[1], ident)
+
+        quantised = quantise_group(nc, pools, frame_rows[0], ident)
+        for c in range(CHUNKS):
+            frame_codes, frame_scales = quantised
+            if c + 1 < CHUNKS:
+                quantised = quantise_group(nc, pools, frame_rows[c + 1], ident)
+
+            half, b0 = c // (SIGNALS // GROUP), GROUP * (c % (SIGNALS // GROUP))
+            real = pools["results"].tile([P, GROUP, N_FFT], F32)
+            minus_imag = pools["results"].tile([P, GROUP, N_FFT], F32)
+            for a in range(GROUP):
+                cols = slice(a * P, (a + 1) * P)
+                cos_product = pools["product"].tile([P, N_FFT], F32, tag="product")
+                nc.tensor.matmul_mx(
+                    out=cos_product[:],
+                    lhsT=frame_codes[:, cols].bitcast(FP8X4),
+                    lhsT_scale=frame_scales[:, cols],
+                    rhs=cos_codes[:].bitcast(FP8X4),
+                    rhs_scale=cos_scales[:],
+                    start=True,
+                    stop=True,
+                )
+                nc.scalar.copy(out=real[:, a, :], in_=cos_product[:])
+                sin_product = pools["product"].tile([P, N_FFT], F32, tag="product")
+                nc.tensor.matmul_mx(
+                    out=sin_product[:],
+                    lhsT=frame_codes[:, cols].bitcast(FP8X4),
+                    lhsT_scale=frame_scales[:, cols],
+                    rhs=sin_codes[:].bitcast(FP8X4),
+                    rhs_scale=sin_scales[:],
+                    start=True,
+                    stop=True,
+                )
+                nc.vector.tensor_scalar_mul(out=minus_imag[:, a, :], in0=sin_product[:], scalar1=-1.0)
+            t_rows = slice(half * P, (half + 1) * P)
+            nc.sync.dma_start(out=out_0[t_rows, b0 : b0 + GROUP, :], in_=real[:])
+            nc.sync.dma_start(out=out_1[t_rows, b0 : b0 + GROUP, :], in_=minus_imag[:])

@@ -12,16 +12,17 @@ FP8X4 = mybir.dt.float8_e4m3fn_x4
 P = 128
 N_FFT = 512
 SIGNALS = 16
-FRAMES = 256
 STRIDE = N_FFT + 1
+RUN = 2 * STRIDE
+RUN_PITCH = 1040
 PACK = 4
 WORDS = N_FFT // 2
 HALVES = WORDS // P
 GROUP = 4
-HALF_FRAMES = FRAMES // P
-CHUNKS = HALF_FRAMES * SIGNALS // GROUP
+LOADS = SIGNALS // GROUP
+CHUNKS = 2 * LOADS
 
-FLOPS = 2 * SIGNALS * FRAMES * N_FFT * (2 * N_FFT)
+FLOPS = 2 * SIGNALS * 2 * P * N_FFT * (2 * N_FFT)
 
 
 def quantise_group(nc, pools, rows, ident):
@@ -33,23 +34,43 @@ def quantise_group(nc, pools, rows, ident):
             row_words = rows[:, 2 * pair + a, :].bitcast(F32)
             for u in range(HALVES):
                 nc.tensor.transpose(flipped[:, a, u, :], row_words[:, u * P : (u + 1) * P], ident[:])
-        source = flipped[:].rearrange("p a u r -> p a r u")
-        target = grouped_words[:, 2 * pair : 2 * pair + 2, :, :]
-        if pair % 2 == 0:
-            nc.scalar.copy(out=target, in_=source)
-        else:
-            nc.vector.tensor_copy(out=target, in_=source)
+        nc.scalar.copy(
+            out=grouped_words[:, 2 * pair : 2 * pair + 2, :, :],
+            in_=flipped[:].rearrange("p a u r -> p a r u"),
+        )
     codes = pools["codes"].tile([P, GROUP * P], U32, align_bytes=64)
     scales = pools["scales"].tile([P, GROUP * P], U8, align_bytes=64)
     nc.vector.quantize_mx(out=codes[:].bitcast(FP8X4), scales=scales[:], in_=grouped[:])
     return codes, scales
 
 
+def multiply_group(nc, pools, frames, weight):
+    frame_codes, frame_scales = frames
+    weight_codes, weight_scales = weight
+    products = []
+    for a in range(GROUP):
+        cols = slice(a * P, (a + 1) * P)
+        product = pools["product"].tile([P, N_FFT], F32)
+        nc.tensor.matmul_mx(
+            out=product[:],
+            lhsT=frame_codes[:, cols].bitcast(FP8X4),
+            lhsT_scale=frame_scales[:, cols],
+            rhs=weight_codes[:].bitcast(FP8X4),
+            rhs_scale=weight_scales[:],
+            start=True,
+            stop=True,
+        )
+        products.append(product)
+    return products
+
+
 def tile_dftlayer_t_kernel(tc, x, wsin, wcos, out_0, out_1):
     nc = tc.nc
     with ExitStack() as ctx:
         pools = {
-            "rows": ctx.enter_context(tc.tile_pool(name="rows", bufs=2 + CHUNKS)),
+            "weights": ctx.enter_context(tc.tile_pool(name="weights", bufs=2)),
+            "runs": ctx.enter_context(tc.tile_pool(name="runs", bufs=LOADS)),
+            "odd": ctx.enter_context(tc.tile_pool(name="odd", bufs=LOADS)),
             "const": ctx.enter_context(tc.tile_pool(name="const", bufs=1)),
             "grouped": ctx.enter_context(tc.tile_pool(name="grouped", bufs=3)),
             "codes": ctx.enter_context(tc.tile_pool(name="codes", bufs=2 + 3)),
@@ -58,61 +79,59 @@ def tile_dftlayer_t_kernel(tc, x, wsin, wcos, out_0, out_1):
             "flipped": ctx.enter_context(tc.psum_pool(name="flipped", bufs=2)),
             "product": ctx.enter_context(tc.psum_pool(name="product", bufs=6)),
         }
+        ctx.enter_context(tc.manual_schedule())
 
-        weight_rows = []
-        for w in (wcos, wsin):
-            rows = pools["rows"].tile([P, GROUP, N_FFT], BF16, tag="rows", name="w_rows")
-            nc.sync.dma_start(out=rows[:], in_=w.rearrange("(a p) n -> p a n", p=P))
-            weight_rows.append(rows)
-        pieces = x[0].rearrange("b (t s) -> t b s", s=STRIDE)
-        frame_rows = []
-        for c in range(CHUNKS):
-            half, b0 = c // (SIGNALS // GROUP), GROUP * (c % (SIGNALS // GROUP))
-            rows = pools["rows"].tile([P, GROUP, N_FFT], BF16, tag="rows", name="x_rows")
+        def load_weight(w):
+            w_rows = pools["weights"].tile([P, GROUP, N_FFT], BF16)
+            nc.sync.dma_start(out=w_rows[:], in_=w.rearrange("(a p) n -> p a n", p=P))
+            return w_rows
+
+        def load_runs(g):
+            runs = pools["runs"].tile([P, GROUP, RUN_PITCH], BF16)
             nc.sync.dma_start(
-                out=rows[:], in_=pieces[half * P : (half + 1) * P, b0 : b0 + GROUP, 0:N_FFT]
+                out=runs[:, :, 0:RUN],
+                in_=x[0].rearrange("b (p s) -> p b s", s=RUN)[:, g * GROUP : (g + 1) * GROUP, :],
             )
-            frame_rows.append(rows)
+            return runs
+
+        sin_rows = load_weight(wsin)
+        all_runs = [load_runs(0)]
+        cos_rows = load_weight(wcos)
+        for g in range(1, LOADS):
+            all_runs.append(load_runs(g))
 
         ident = pools["const"].tile([P, P], F32)
         make_identity(nc, ident[:])
 
-        cos_codes, cos_scales = quantise_group(nc, pools, weight_rows[0], ident)
-        sin_codes, sin_scales = quantise_group(nc, pools, weight_rows[1], ident)
+        chunk_rows = [runs[:, :, 0:N_FFT] for runs in all_runs]
 
-        quantised = quantise_group(nc, pools, frame_rows[0], ident)
+        sin_weight = quantise_group(nc, pools, sin_rows[:], ident)
+        frames = quantise_group(nc, pools, chunk_rows[0], ident)
+        cos_weight = quantise_group(nc, pools, cos_rows[:], ident)
+
+        real_view = out_0.rearrange("(p two) b k -> p two b k", two=2)
+        minus_imag_view = out_1.rearrange("(p two) b k -> p two b k", two=2)
+
         for c in range(CHUNKS):
-            frame_codes, frame_scales = quantised
-            if c + 1 < CHUNKS:
-                quantised = quantise_group(nc, pools, frame_rows[c + 1], ident)
+            parity, g = c // LOADS, c % LOADS
+            signals = slice(g * GROUP, (g + 1) * GROUP)
 
-            half, b0 = c // (SIGNALS // GROUP), GROUP * (c % (SIGNALS // GROUP))
-            real = pools["results"].tile([P, GROUP, N_FFT], F32)
+            sin_products = multiply_group(nc, pools, frames, sin_weight)
             minus_imag = pools["results"].tile([P, GROUP, N_FFT], F32)
             for a in range(GROUP):
-                cols = slice(a * P, (a + 1) * P)
-                cos_product = pools["product"].tile([P, N_FFT], F32, tag="product")
-                nc.tensor.matmul_mx(
-                    out=cos_product[:],
-                    lhsT=frame_codes[:, cols].bitcast(FP8X4),
-                    lhsT_scale=frame_scales[:, cols],
-                    rhs=cos_codes[:].bitcast(FP8X4),
-                    rhs_scale=cos_scales[:],
-                    start=True,
-                    stop=True,
-                )
-                nc.scalar.copy(out=real[:, a, :], in_=cos_product[:])
-                sin_product = pools["product"].tile([P, N_FFT], F32, tag="product")
-                nc.tensor.matmul_mx(
-                    out=sin_product[:],
-                    lhsT=frame_codes[:, cols].bitcast(FP8X4),
-                    lhsT_scale=frame_scales[:, cols],
-                    rhs=sin_codes[:].bitcast(FP8X4),
-                    rhs_scale=sin_scales[:],
-                    start=True,
-                    stop=True,
-                )
-                nc.vector.tensor_scalar_mul(out=minus_imag[:, a, :], in0=sin_product[:], scalar1=-1.0)
-            t_rows = slice(half * P, (half + 1) * P)
-            nc.sync.dma_start(out=out_0[t_rows, b0 : b0 + GROUP, :], in_=real[:])
-            nc.sync.dma_start(out=out_1[t_rows, b0 : b0 + GROUP, :], in_=minus_imag[:])
+                nc.vector.tensor_scalar_mul(out=minus_imag[:, a, :], in0=sin_products[a][:], scalar1=-1.0)
+            nc.sync.dma_start(out=minus_imag_view[:, parity, signals, :], in_=minus_imag[:])
+
+            this_frames = frames
+            if c + 1 < CHUNKS:
+                frames = quantise_group(nc, pools, chunk_rows[c + 1], ident)
+            if parity == 0:
+                odd = pools["odd"].tile([P, GROUP, N_FFT], BF16)
+                nc.vector.tensor_copy(out=odd[:], in_=all_runs[g][:, :, STRIDE : STRIDE + N_FFT])
+                chunk_rows.append(odd[:])
+
+            cos_products = multiply_group(nc, pools, this_frames, cos_weight)
+            real = pools["results"].tile([P, GROUP, N_FFT], F32)
+            for a in range(GROUP):
+                nc.scalar.copy(out=real[:, a, :], in_=cos_products[a][:])
+            nc.sync.dma_start(out=real_view[:, parity, signals, :], in_=real[:])

@@ -14,7 +14,6 @@ N_FFT = 512
 SIGNALS = 16
 STRIDE = N_FFT + 1
 RUN = 2 * STRIDE
-RUN_PITCH = 1040
 PACK = 4
 WORDS = N_FFT // 2
 HALVES = WORDS // P
@@ -69,8 +68,7 @@ def tile_dftlayer_t_kernel(tc, x, wsin, wcos, out_0, out_1):
     with ExitStack() as ctx:
         pools = {
             "weights": ctx.enter_context(tc.tile_pool(name="weights", bufs=2)),
-            "runs": ctx.enter_context(tc.tile_pool(name="runs", bufs=LOADS)),
-            "odd": ctx.enter_context(tc.tile_pool(name="odd", bufs=LOADS)),
+            "runs": ctx.enter_context(tc.tile_pool(name="runs", bufs=CHUNKS)),
             "const": ctx.enter_context(tc.tile_pool(name="const", bufs=1)),
             "grouped": ctx.enter_context(tc.tile_pool(name="grouped", bufs=3)),
             "codes": ctx.enter_context(tc.tile_pool(name="codes", bufs=2 + 3)),
@@ -86,24 +84,29 @@ def tile_dftlayer_t_kernel(tc, x, wsin, wcos, out_0, out_1):
             nc.sync.dma_start(out=w_rows[:], in_=w.rearrange("(a p) n -> p a n", p=P))
             return w_rows
 
-        def load_runs(g):
-            runs = pools["runs"].tile([P, GROUP, RUN_PITCH], BF16)
+        def load_runs(g, parity):
+            runs = pools["runs"].tile([P, GROUP, N_FFT], BF16)
+            start = parity * STRIDE
             nc.sync.dma_start(
-                out=runs[:, :, 0:RUN],
-                in_=x[0].rearrange("b (p s) -> p b s", s=RUN)[:, g * GROUP : (g + 1) * GROUP, :],
+                out=runs[:],
+                in_=x[0].rearrange("b (p s) -> p b s", s=RUN)[
+                    :, g * GROUP : (g + 1) * GROUP, start : start + N_FFT
+                ],
             )
             return runs
 
         sin_rows = load_weight(wsin)
-        all_runs = [load_runs(0)]
+        even_runs = [load_runs(0, 0)]
+        odd_runs = [load_runs(0, 1)]
         cos_rows = load_weight(wcos)
         for g in range(1, LOADS):
-            all_runs.append(load_runs(g))
+            even_runs.append(load_runs(g, 0))
+            odd_runs.append(load_runs(g, 1))
 
         ident = pools["const"].tile([P, P], F32)
         make_identity(nc, ident[:])
 
-        chunk_rows = [runs[:, :, 0:N_FFT] for runs in all_runs]
+        chunk_rows = [runs[:] for runs in even_runs + odd_runs]
 
         sin_weight = quantise_group(nc, pools, sin_rows[:], ident)
         frames = quantise_group(nc, pools, chunk_rows[0], ident)
@@ -125,10 +128,6 @@ def tile_dftlayer_t_kernel(tc, x, wsin, wcos, out_0, out_1):
             this_frames = frames
             if c + 1 < CHUNKS:
                 frames = quantise_group(nc, pools, chunk_rows[c + 1], ident)
-            if parity == 0:
-                odd = pools["odd"].tile([P, GROUP, N_FFT], BF16)
-                nc.vector.tensor_copy(out=odd[:], in_=all_runs[g][:, :, STRIDE : STRIDE + N_FFT])
-                chunk_rows.append(odd[:])
 
             cos_products = multiply_group(nc, pools, this_frames, cos_weight)
             real = pools["results"].tile([P, GROUP, N_FFT], F32)

from contextlib import ExitStack

import concourse.mybir as mybir
from concourse.masks import make_identity

F32 = mybir.dt.float32
BF16 = mybir.dt.bfloat16
U32 = mybir.dt.uint32
U8 = mybir.dt.uint8
FP8X4 = mybir.dt.float8_e4m3fn_x4

P = 128
N_FFT = 512
SIGNALS = 16
STRIDE = N_FFT + 1
RUN = 2 * STRIDE
PACK = 4
WORDS = N_FFT // 2
HALVES = WORDS // P
GROUP = 4
LOADS = SIGNALS // GROUP
CHUNKS = 2 * LOADS

FLOPS = 2 * SIGNALS * 2 * P * N_FFT * (2 * N_FFT)


def quantise_group(nc, pools, rows, ident):
    grouped = pools["grouped"].tile([P, GROUP * P * PACK], BF16, align_bytes=64)
    grouped_words = grouped[:].bitcast(F32).rearrange("p (a r u) -> p a r u", a=GROUP, u=HALVES)
    for pair in range(GROUP // 2):
        flipped = pools["flipped"].tile([P, 2, HALVES, P], F32)
        for a in range(2):
            row_words = rows[:, 2 * pair + a, :].bitcast(F32)
            for u in range(HALVES):
                nc.tensor.transpose(flipped[:, a, u, :], row_words[:, u * P : (u + 1) * P], ident[:])
        nc.scalar.copy(
            out=grouped_words[:, 2 * pair : 2 * pair + 2, :, :],
            in_=flipped[:].rearrange("p a u r -> p a r u"),
        )
    codes = pools["codes"].tile([P, GROUP * P], U32, align_bytes=64)
    scales = pools["scales"].tile([P, GROUP * P], U8, align_bytes=64)
    nc.vector.quantize_mx(out=codes[:].bitcast(FP8X4), scales=scales[:], in_=grouped[:])
    return codes, scales


def multiply_group(nc, pools, frames, weight):
    frame_codes, frame_scales = frames
    weight_codes, weight_scales = weight
    products = []
    for a in range(GROUP):
        cols = slice(a * P, (a + 1) * P)
        product = pools["product"].tile([P, N_FFT], F32)
        nc.tensor.matmul_mx(
            out=product[:],
            lhsT=frame_codes[:, cols].bitcast(FP8X4),
            lhsT_scale=frame_scales[:, cols],
            rhs=weight_codes[:].bitcast(FP8X4),
            rhs_scale=weight_scales[:],
            start=True,
            stop=True,
        )
        products.append(product)
    return products


def tile_dftlayer_t_kernel(tc, x, wsin, wcos, out_0, out_1):
    nc = tc.nc
    with ExitStack() as ctx:
        pools = {
            "weights": ctx.enter_context(tc.tile_pool(name="weights", bufs=2)),
            "runs": ctx.enter_context(tc.tile_pool(name="runs", bufs=CHUNKS)),
            "const": ctx.enter_context(tc.tile_pool(name="const", bufs=1)),
            "grouped": ctx.enter_context(tc.tile_pool(name="grouped", bufs=3)),
            "codes": ctx.enter_context(tc.tile_pool(name="codes", bufs=2 + 3)),
            "scales": ctx.enter_context(tc.tile_pool(name="scales", bufs=2 + 3)),
            "results": ctx.enter_context(tc.tile_pool(name="results", bufs=CHUNKS)),
            "flipped": ctx.enter_context(tc.psum_pool(name="flipped", bufs=2)),
            "product": ctx.enter_context(tc.psum_pool(name="product", bufs=6)),
        }
        ctx.enter_context(tc.manual_schedule())

        def load_weight(w):
            w_rows = pools["weights"].tile([P, GROUP, N_FFT], BF16)
            nc.sync.dma_start(out=w_rows[:], in_=w.rearrange("(a p) n -> p a n", p=P))
            return w_rows

        def load_runs(g, parity):
            runs = pools["runs"].tile([P, GROUP, N_FFT], BF16)
            start = parity * STRIDE
            nc.sync.dma_start(
                out=runs[:],
                in_=x[0].rearrange("b (p s) -> p b s", s=RUN)[
                    :, g * GROUP : (g + 1) * GROUP, start : start + N_FFT
                ],
            )
            return runs

        sin_rows = load_weight(wsin)
        even_runs = [load_runs(0, 0)]
        odd_runs = [load_runs(0, 1)]
        cos_rows = load_weight(wcos)
        for g in range(1, LOADS):
            even_runs.append(load_runs(g, 0))
            odd_runs.append(load_runs(g, 1))

        ident = pools["const"].tile([P, P], F32)
        make_identity(nc, ident[:])

        chunk_rows = [runs[:] for runs in even_runs + odd_runs]

        sin_weight = quantise_group(nc, pools, sin_rows[:], ident)
        frames = quantise_group(nc, pools, chunk_rows[0], ident)
        cos_weight = quantise_group(nc, pools, cos_rows[:], ident)

        real_view = out_0.rearrange("(p two) b k -> p two b k", two=2)
        minus_imag_view = out_1.rearrange("(p two) b k -> p two b k", two=2)

        for c in range(CHUNKS):
            parity, g = c // LOADS, c % LOADS
            signals = slice(g * GROUP, (g + 1) * GROUP)

            sin_products = multiply_group(nc, pools, frames, sin_weight)
            minus_imag = pools["results"].tile([P, GROUP, N_FFT], F32)
            for a in range(GROUP):
                nc.vector.tensor_scalar_mul(out=minus_imag[:, a, :], in0=sin_products[a][:], scalar1=-1.0)
            nc.sync.dma_start(out=minus_imag_view[:, parity, signals, :], in_=minus_imag[:])

            this_frames = frames
            if c + 1 < CHUNKS:
                frames = quantise_group(nc, pools, chunk_rows[c + 1], ident)

            cos_products = multiply_group(nc, pools, this_frames, cos_weight)
            real = pools["results"].tile([P, GROUP, N_FFT], F32)
            for a in range(GROUP):
                nc.scalar.copy(out=real[:, a, :], in_=cos_products[a][:])
            nc.sync.dma_start(out=real_view[:, parity, signals, :], in_=real[:])
